import numpy as np
import ml_dtypes

BF16 = ml_dtypes.bfloat16


def bf(x):
    return np.asarray(x, np.float32).astype(BF16)


def f32(x):
    return np.asarray(x, np.float32)


def f64(x):
    return np.asarray(x).astype(np.float64)


def striped(idx):
    return np.tile(idx.reshape(-1, 16).T, (8, 1))


C, S, N, H, HD = 512, 2048, 512, 4, 128


def silu(v):
    return v / (1.0 + np.exp(-v))


def setup_inputs():
    return {
        "base": f32(np.random.standard_normal((C, S))),
        "gate": f32(np.random.standard_normal((C, N))),
        "up": f32(np.random.standard_normal((C, N))),
        "adj_t": bf(np.random.uniform(size=(H, N, N)) * (2.0 / np.sqrt(N))),
        "eps": f32(np.repeat(0.1 + 0.2 * np.random.uniform(size=H), HD)[:, None]),
        "alpha": f32(np.repeat(1.1 + 0.3 * np.random.uniform(size=H), HD)[:, None]),
        "offs": striped(np.random.permutation(S)[:N]),
    }


def reference(base, gate, up, adj_t, eps, alpha, offs):
    idx = offs[:16].T.reshape(-1)
    hid = silu(f64(gate)) * f64(up)
    agg = np.einsum("qdt,qts->qds", hid.reshape(H, HD, N), f64(adj_t)).reshape(C, N)
    out = f64(base).copy()
    out[:, idx] = (1.0 + f64(eps)) * hid + f64(alpha) * agg
    return out

@@ -1,0 +1,73 @@
+import concourse.mybir as mybir
+from concourse.masks import make_identity
+
+F32, BF16, U16 = mybir.dt.float32, mybir.dt.bfloat16, mybir.dt.uint16
+MULT, ADD = mybir.AluOpType.mult, mybir.AluOpType.add
+SILU, COPY = mybir.ActivationFunctionType.Silu, mybir.ActivationFunctionType.Copy
+
+P = 128
+HEADS = 4
+TOKENS = 512
+SLOTS = 2048
+CHUNKS = TOKENS // P
+
+FLOPS = 2 * HEADS * P * TOKENS * TOKENS
+
+
+def tile_llamamlp_halfwaygin_kernel(tc, base, gate, up, adj_t, eps, alpha, offs, out):
+    nc = tc.nc
+    with (
+        tc.tile_pool(name="held", bufs=1) as held,
+        tc.tile_pool(name="loads", bufs=HEADS) as loads,
+        tc.tile_pool(name="work", bufs=2) as work,
+        tc.psum_pool(name="psum", bufs=2) as psum,
+    ):
+        offsets = held.tile([P, TOKENS // 16], U16, name="offsets")
+        nc.sync.dma_start(offsets[:], offs)
+
+        eps_cols = held.tile([P, HEADS], F32, name="eps_cols")
+        alpha_cols = held.tile([P, HEADS], F32, name="alpha_cols")
+        with nc.allow_non_contiguous_dma(reason="one float32 a partition and head: 512 elements in all"):
+            nc.scalar.dma_start(eps_cols[:], eps.rearrange("(q p) o -> p (q o)", p=P))
+            nc.scalar.dma_start(alpha_cols[:], alpha.rearrange("(q p) o -> p (q o)", p=P))
+        one_plus_eps = held.tile([P, HEADS], F32, name="one_plus_eps")
+        nc.vector.tensor_scalar_add(one_plus_eps[:], eps_cols[:], 1.0)
+
+        identity = held.tile([P, P], BF16, name="identity")
+        make_identity(nc, identity[:])
+
+        for q in range(HEADS):
+            rows = slice(q * P, (q + 1) * P)
+            gate_q = loads.tile([P, TOKENS], F32, name="gate_q")
+            up_q = loads.tile([P, TOKENS], F32, name="up_q")
+            adj_q = loads.tile([P, CHUNKS, TOKENS], BF16, name="adj_q")
+            window = loads.tile([P, SLOTS], F32, name="window")
+            nc.sync.dma_start(gate_q[:], gate[rows, :])
+            nc.sync.dma_start(up_q[:], up[rows, :])
+            nc.sync.dma_start(adj_q[:], adj_t[q].rearrange("(k p) j -> p k j", p=P))
+            nc.sync.dma_start(window[:], base[rows, :])
+
+            silu_q = work.tile([P, TOKENS], F32, name="silu_q")
+            nc.scalar.activation(silu_q[:], gate_q[:], SILU)
+            hid_bf = work.tile([P, TOKENS], BF16, name="hid_bf")
+            nc.vector.tensor_tensor(hid_bf[:], silu_q[:], up_q[:], MULT)
+            own = work.tile([P, TOKENS], F32, name="own")
+            nc.vector.scalar_tensor_tensor(own[:], silu_q[:], one_plus_eps[:, q : q + 1], up_q[:], MULT, MULT)
+
+            hid_t_ps = psum.tile([P, TOKENS], BF16, name="hid_t_ps")
+            for k in range(CHUNKS):
+                cols = slice(k * P, (k + 1) * P)
+                nc.tensor.transpose(hid_t_ps[:, cols], hid_bf[:, cols], identity[:])
+            hid_t = work.tile([P, TOKENS], BF16, name="hid_t")
+            nc.scalar.copy(hid_t[:], hid_t_ps[:])
+
+            agg_ps = psum.tile([P, TOKENS], F32, name="agg_ps")
+            for k in range(CHUNKS):
+                nc.tensor.matmul(
+                    agg_ps[:], hid_t[:, k * P : (k + 1) * P], adj_q[:, k, :], start=(k == 0), stop=(k == CHUNKS - 1)
+                )
+            mixed = work.tile([P, TOKENS], F32, name="mixed")
+            nc.scalar.activation(mixed[:], agg_ps[:], COPY, scale=alpha_cols[:, q : q + 1])
+
+            nc.vector.tensor_tensor(window[:].indirect(offsets[:]), own[:], mixed[:], ADD)
+            nc.sync.dma_start(out[rows, :], window[:])

@@ -36,16 +36,21 @@ def tile_llamamlp_halfwaygin_kernel(tc, base, gate, up, adj_t, eps, alpha, offs,
         identity = held.tile([P, P], BF16, name="identity")
         make_identity(nc, identity[:])
 
+        gates, ups, adjs, windows = [], [], [], []
         for q in range(HEADS):
             rows = slice(q * P, (q + 1) * P)
-            gate_q = loads.tile([P, TOKENS], F32, name="gate_q")
-            up_q = loads.tile([P, TOKENS], F32, name="up_q")
-            adj_q = loads.tile([P, CHUNKS, TOKENS], BF16, name="adj_q")
-            window = loads.tile([P, SLOTS], F32, name="window")
-            nc.sync.dma_start(gate_q[:], gate[rows, :])
-            nc.sync.dma_start(up_q[:], up[rows, :])
-            nc.sync.dma_start(adj_q[:], adj_t[q].rearrange("(k p) j -> p k j", p=P))
-            nc.sync.dma_start(window[:], base[rows, :])
+            gates.append(loads.tile([P, TOKENS], F32, name="gate_q"))
+            ups.append(loads.tile([P, TOKENS], F32, name="up_q"))
+            adjs.append(loads.tile([P, CHUNKS, TOKENS], BF16, name="adj_q"))
+            windows.append(loads.tile([P, SLOTS], F32, name="window"))
+            nc.sync.dma_start(gates[q][:], gate[rows, :])
+            nc.sync.dma_start(ups[q][:], up[rows, :])
+            nc.sync.dma_start(adjs[q][:], adj_t[q].rearrange("(k p) j -> p k j", p=P))
+            nc.sync.dma_start(windows[q][:], base[rows, :])
+
+        for q in range(HEADS):
+            rows = slice(q * P, (q + 1) * P)
+            gate_q, up_q, adj_q, window = gates[q], ups[q], adjs[q], windows[q]
 
             silu_q = work.tile([P, TOKENS], F32, name="silu_q")
             nc.scalar.activation(silu_q[:], gate_q[:], SILU)

@@ -18,9 +18,8 @@ def tile_llamamlp_halfwaygin_kernel(tc, base, gate, up, adj_t, eps, alpha, offs,
     nc = tc.nc
     with (
         tc.tile_pool(name="held", bufs=1) as held,
-        tc.tile_pool(name="loads", bufs=HEADS) as loads,
-        tc.tile_pool(name="work", bufs=2) as work,
-        tc.psum_pool(name="psum", bufs=2) as psum,
+        tc.tile_pool(name="per_head", bufs=HEADS) as per_head,
+        tc.psum_pool(name="psum", bufs=HEADS) as psum,
     ):
         offsets = held.tile([P, TOKENS // 16], U16, name="offsets")
         nc.sync.dma_start(offsets[:], offs)
@@ -36,43 +35,41 @@ def tile_llamamlp_halfwaygin_kernel(tc, base, gate, up, adj_t, eps, alpha, offs,
         identity = held.tile([P, P], BF16, name="identity")
         make_identity(nc, identity[:])
 
+        head_rows = [slice(q * P, (q + 1) * P) for q in range(HEADS)]
         gates, ups, adjs, windows = [], [], [], []
         for q in range(HEADS):
-            rows = slice(q * P, (q + 1) * P)
-            gates.append(loads.tile([P, TOKENS], F32, name="gate_q"))
-            ups.append(loads.tile([P, TOKENS], F32, name="up_q"))
-            adjs.append(loads.tile([P, CHUNKS, TOKENS], BF16, name="adj_q"))
-            windows.append(loads.tile([P, SLOTS], F32, name="window"))
-            nc.sync.dma_start(gates[q][:], gate[rows, :])
-            nc.sync.dma_start(ups[q][:], up[rows, :])
-            nc.sync.dma_start(adjs[q][:], adj_t[q].rearrange("(k p) j -> p k j", p=P))
-            nc.sync.dma_start(windows[q][:], base[rows, :])
-
+            gates.append(per_head.tile([P, TOKENS], F32, name="gate_q"))
+            ups.append(per_head.tile([P, TOKENS], F32, name="up_q"))
+            nc.sync.dma_start(gates[q][:], gate[head_rows[q], :])
+            nc.sync.dma_start(ups[q][:], up[head_rows[q], :])
         for q in range(HEADS):
-            rows = slice(q * P, (q + 1) * P)
-            gate_q, up_q, adj_q, window = gates[q], ups[q], adjs[q], windows[q]
+            adjs.append(per_head.tile([P, CHUNKS, TOKENS], BF16, name="adj_q"))
+            windows.append(per_head.tile([P, SLOTS], F32, name="window"))
+            nc.sync.dma_start(adjs[q][:], adj_t[q].rearrange("(k p) j -> p k j", p=P))
+            nc.sync.dma_start(windows[q][:], base[head_rows[q], :])
 
-            silu_q = work.tile([P, TOKENS], F32, name="silu_q")
-            nc.scalar.activation(silu_q[:], gate_q[:], SILU)
-            hid_bf = work.tile([P, TOKENS], BF16, name="hid_bf")
-            nc.vector.tensor_tensor(hid_bf[:], silu_q[:], up_q[:], MULT)
-            own = work.tile([P, TOKENS], F32, name="own")
-            nc.vector.scalar_tensor_tensor(own[:], silu_q[:], one_plus_eps[:, q : q + 1], up_q[:], MULT, MULT)
-
+        owns, hid_ts = [], []
+        for q in range(HEADS):
+            silu_q = per_head.tile([P, TOKENS], F32, name="silu_q")
+            nc.scalar.activation(silu_q[:], gates[q][:], SILU)
+            hid_bf = per_head.tile([P, TOKENS], BF16, name="hid_bf")
+            nc.vector.tensor_tensor(hid_bf[:], silu_q[:], ups[q][:], MULT)
+            owns.append(per_head.tile([P, TOKENS], F32, name="own"))
+            nc.vector.scalar_tensor_tensor(owns[q][:], silu_q[:], one_plus_eps[:, q : q + 1], ups[q][:], MULT, MULT)
             hid_t_ps = psum.tile([P, TOKENS], BF16, name="hid_t_ps")
             for k in range(CHUNKS):
                 cols = slice(k * P, (k + 1) * P)
                 nc.tensor.transpose(hid_t_ps[:, cols], hid_bf[:, cols], identity[:])
-            hid_t = work.tile([P, TOKENS], BF16, name="hid_t")
-            nc.scalar.copy(hid_t[:], hid_t_ps[:])
+            hid_ts.append(per_head.tile([P, TOKENS], BF16, name="hid_t"))
+            nc.scalar.copy(hid_ts[q][:], hid_t_ps[:])
 
+        for q in range(HEADS):
             agg_ps = psum.tile([P, TOKENS], F32, name="agg_ps")
             for k in range(CHUNKS):
                 nc.tensor.matmul(
-                    agg_ps[:], hid_t[:, k * P : (k + 1) * P], adj_q[:, k, :], start=(k == 0), stop=(k == CHUNKS - 1)
+                    agg_ps[:], hid_ts[q][:, k * P : (k + 1) * P], adjs[q][:, k, :], start=(k == 0), stop=(k == CHUNKS - 1)
                 )
-            mixed = work.tile([P, TOKENS], F32, name="mixed")
+            mixed = per_head.tile([P, TOKENS], F32, name="mixed")
             nc.scalar.activation(mixed[:], agg_ps[:], COPY, scale=alpha_cols[:, q : q + 1])
-
-            nc.vector.tensor_tensor(window[:].indirect(offsets[:]), own[:], mixed[:], ADD)
-            nc.sync.dma_start(out[rows, :], window[:])
+            nc.vector.tensor_tensor(windows[q][:].indirect(offsets[:]), owns[q][:], mixed[:], ADD)
+            nc.sync.dma_start(out[head_rows[q], :], windows[q][:])

@@ -45,7 +45,7 @@ def tile_llamamlp_halfwaygin_kernel(tc, base, gate, up, adj_t, eps, alpha, offs,
         for q in range(HEADS):
             adjs.append(per_head.tile([P, CHUNKS, TOKENS], BF16, name="adj_q"))
             windows.append(per_head.tile([P, SLOTS], F32, name="window"))
-            nc.sync.dma_start(adjs[q][:], adj_t[q].rearrange("(k p) j -> p k j", p=P))
+            nc.sync.dma_start(adjs[q][:], adj_t[q].rearrange("(p k) j -> p k j", p=P))
             nc.sync.dma_start(windows[q][:], base[head_rows[q], :])
 
         owns, hid_ts = [], []
@@ -57,9 +57,9 @@ def tile_llamamlp_halfwaygin_kernel(tc, base, gate, up, adj_t, eps, alpha, offs,
             owns.append(per_head.tile([P, TOKENS], F32, name="own"))
             nc.vector.scalar_tensor_tensor(owns[q][:], silu_q[:], one_plus_eps[:, q : q + 1], ups[q][:], MULT, MULT)
             hid_t_ps = psum.tile([P, TOKENS], BF16, name="hid_t_ps")
+            hid_by_chunk = hid_bf[:].rearrange("c (p k) -> c k p", k=CHUNKS)
             for k in range(CHUNKS):
-                cols = slice(k * P, (k + 1) * P)
-                nc.tensor.transpose(hid_t_ps[:, cols], hid_bf[:, cols], identity[:])
+                nc.tensor.transpose(hid_t_ps[:, k * P : (k + 1) * P], hid_by_chunk[:, k, :], identity[:])
             hid_ts.append(per_head.tile([P, TOKENS], BF16, name="hid_t"))
             nc.scalar.copy(hid_ts[q][:], hid_t_ps[:])
 

@@ -10,6 +10,7 @@ HEADS = 4
 TOKENS = 512
 SLOTS = 2048
 CHUNKS = TOKENS // P
+SCALE_ROWS = 64
 
 FLOPS = 2 * HEADS * P * TOKENS * TOKENS
 
@@ -19,21 +20,28 @@ def tile_llamamlp_halfwaygin_kernel(tc, base, gate, up, adj_t, eps, alpha, offs,
     with (
         tc.tile_pool(name="held", bufs=1) as held,
         tc.tile_pool(name="per_head", bufs=HEADS) as per_head,
-        tc.psum_pool(name="psum", bufs=HEADS) as psum,
+        tc.psum_pool(name="psum_scales", bufs=1) as psum_scales,
+        tc.psum_pool(name="psum_hid_t", bufs=2) as psum_hid_t,
+        tc.psum_pool(name="psum_agg", bufs=HEADS) as psum_agg,
     ):
         offsets = held.tile([P, TOKENS // 16], U16, name="offsets")
         nc.sync.dma_start(offsets[:], offs)
 
-        eps_cols = held.tile([P, HEADS], F32, name="eps_cols")
-        alpha_cols = held.tile([P, HEADS], F32, name="alpha_cols")
-        with nc.allow_non_contiguous_dma(reason="one float32 a partition and head: 512 elements in all"):
-            nc.scalar.dma_start(eps_cols[:], eps.rearrange("(q p) o -> p (q o)", p=P))
-            nc.scalar.dma_start(alpha_cols[:], alpha.rearrange("(q p) o -> p (q o)", p=P))
-        one_plus_eps = held.tile([P, HEADS], F32, name="one_plus_eps")
-        nc.vector.tensor_scalar_add(one_plus_eps[:], eps_cols[:], 1.0)
-
         identity = held.tile([P, P], BF16, name="identity")
         make_identity(nc, identity[:])
+
+        scale_rows = held.tile([SCALE_ROWS, P], F32, name="scale_rows")
+        nc.vector.memset(scale_rows[:], 0.0)
+        nc.scalar.dma_start(scale_rows[0:HEADS, :], eps.rearrange("(q p) o -> q (p o)", p=P))
+        nc.scalar.dma_start(scale_rows[HEADS : 2 * HEADS, :], alpha.rearrange("(q p) o -> q (p o)", p=P))
+        identity_f32 = held.tile([SCALE_ROWS, SCALE_ROWS], F32, name="identity_f32")
+        make_identity(nc, identity_f32[:])
+        scale_cols_ps = psum_scales.tile([P, SCALE_ROWS], F32, name="scale_cols_ps")
+        nc.tensor.transpose(scale_cols_ps[:], scale_rows[:], identity_f32[:])
+        one_plus_eps = held.tile([P, HEADS], F32, name="one_plus_eps")
+        nc.vector.tensor_scalar_add(one_plus_eps[:], scale_cols_ps[:, 0:HEADS], 1.0)
+        alpha_cols = held.tile([P, HEADS], F32, name="alpha_cols")
+        nc.vector.tensor_copy(alpha_cols[:], scale_cols_ps[:, HEADS : 2 * HEADS])
 
         head_rows = [slice(q * P, (q + 1) * P) for q in range(HEADS)]
         gates, ups, adjs, windows = [], [], [], []
@@ -45,7 +53,7 @@ def tile_llamamlp_halfwaygin_kernel(tc, base, gate, up, adj_t, eps, alpha, offs,
         for q in range(HEADS):
             adjs.append(per_head.tile([P, CHUNKS, TOKENS], BF16, name="adj_q"))
             windows.append(per_head.tile([P, SLOTS], F32, name="window"))
-            nc.sync.dma_start(adjs[q][:], adj_t[q].rearrange("(p k) j -> p k j", p=P))
+            nc.sync.dma_start(adjs[q][:], adj_t[q].rearrange("(k p) j -> p k j", p=P))
             nc.sync.dma_start(windows[q][:], base[head_rows[q], :])
 
         owns, hid_ts = [], []
@@ -56,15 +64,15 @@ def tile_llamamlp_halfwaygin_kernel(tc, base, gate, up, adj_t, eps, alpha, offs,
             nc.vector.tensor_tensor(hid_bf[:], silu_q[:], ups[q][:], MULT)
             owns.append(per_head.tile([P, TOKENS], F32, name="own"))
             nc.vector.scalar_tensor_tensor(owns[q][:], silu_q[:], one_plus_eps[:, q : q + 1], ups[q][:], MULT, MULT)
-            hid_t_ps = psum.tile([P, TOKENS], BF16, name="hid_t_ps")
-            hid_by_chunk = hid_bf[:].rearrange("c (p k) -> c k p", k=CHUNKS)
+            hid_t_ps = psum_hid_t.tile([P, TOKENS], BF16, name="hid_t_ps")
             for k in range(CHUNKS):
-                nc.tensor.transpose(hid_t_ps[:, k * P : (k + 1) * P], hid_by_chunk[:, k, :], identity[:])
+                cols = slice(k * P, (k + 1) * P)
+                nc.tensor.transpose(hid_t_ps[:, cols], hid_bf[:, cols], identity[:])
             hid_ts.append(per_head.tile([P, TOKENS], BF16, name="hid_t"))
             nc.scalar.copy(hid_ts[q][:], hid_t_ps[:])
 
         for q in range(HEADS):
-            agg_ps = psum.tile([P, TOKENS], F32, name="agg_ps")
+            agg_ps = psum_agg.tile([P, TOKENS], F32, name="agg_ps")
             for k in range(CHUNKS):
                 nc.tensor.matmul(
                     agg_ps[:], hid_ts[q][:, k * P : (k + 1) * P], adjs[q][:, k, :], start=(k == 0), stop=(k == CHUNKS - 1)

@@ -27,8 +27,18 @@ def tile_llamamlp_halfwaygin_kernel(tc, base, gate, up, adj_t, eps, alpha, offs,
         offsets = held.tile([P, TOKENS // 16], U16, name="offsets")
         nc.sync.dma_start(offsets[:], offs)
 
-        identity = held.tile([P, P], BF16, name="identity")
-        make_identity(nc, identity[:])
+        head_rows = [slice(q * P, (q + 1) * P) for q in range(HEADS)]
+        gates, ups, adjs, windows = [], [], [], []
+        for q in range(HEADS):
+            gates.append(per_head.tile([P, TOKENS], F32, name="gate_q"))
+            ups.append(per_head.tile([P, TOKENS], F32, name="up_q"))
+            nc.sync.dma_start(gates[q][:], gate[head_rows[q], :])
+            nc.sync.dma_start(ups[q][:], up[head_rows[q], :])
+        for q in range(HEADS):
+            adjs.append(per_head.tile([P, CHUNKS, TOKENS], BF16, name="adj_q"))
+            windows.append(per_head.tile([P, SLOTS], F32, name="window"))
+            nc.sync.dma_start(adjs[q][:], adj_t[q].rearrange("(p k) j -> p k j", p=P))
+            nc.sync.dma_start(windows[q][:], base[head_rows[q], :])
 
         scale_rows = held.tile([SCALE_ROWS, P], F32, name="scale_rows")
         nc.vector.memset(scale_rows[:], 0.0)
@@ -43,40 +53,31 @@ def tile_llamamlp_halfwaygin_kernel(tc, base, gate, up, adj_t, eps, alpha, offs,
         alpha_cols = held.tile([P, HEADS], F32, name="alpha_cols")
         nc.vector.tensor_copy(alpha_cols[:], scale_cols_ps[:, HEADS : 2 * HEADS])
 
-        head_rows = [slice(q * P, (q + 1) * P) for q in range(HEADS)]
-        gates, ups, adjs, windows = [], [], [], []
-        for q in range(HEADS):
-            gates.append(per_head.tile([P, TOKENS], F32, name="gate_q"))
-            ups.append(per_head.tile([P, TOKENS], F32, name="up_q"))
-            nc.sync.dma_start(gates[q][:], gate[head_rows[q], :])
-            nc.sync.dma_start(ups[q][:], up[head_rows[q], :])
-        for q in range(HEADS):
-            adjs.append(per_head.tile([P, CHUNKS, TOKENS], BF16, name="adj_q"))
-            windows.append(per_head.tile([P, SLOTS], F32, name="window"))
-            nc.sync.dma_start(adjs[q][:], adj_t[q].rearrange("(k p) j -> p k j", p=P))
-            nc.sync.dma_start(windows[q][:], base[head_rows[q], :])
+        identity_bf = held.tile([P, P], BF16, name="identity_bf")
+        make_identity(nc, identity_bf[:])
 
-        owns, hid_ts = [], []
+        silus, hid_bfs = [], []
         for q in range(HEADS):
-            silu_q = per_head.tile([P, TOKENS], F32, name="silu_q")
-            nc.scalar.activation(silu_q[:], gates[q][:], SILU)
-            hid_bf = per_head.tile([P, TOKENS], BF16, name="hid_bf")
-            nc.vector.tensor_tensor(hid_bf[:], silu_q[:], ups[q][:], MULT)
-            owns.append(per_head.tile([P, TOKENS], F32, name="own"))
-            nc.vector.scalar_tensor_tensor(owns[q][:], silu_q[:], one_plus_eps[:, q : q + 1], ups[q][:], MULT, MULT)
-            hid_t_ps = psum_hid_t.tile([P, TOKENS], BF16, name="hid_t_ps")
+            silus.append(per_head.tile([P, TOKENS], F32, name="silu_q"))
+            nc.scalar.activation(silus[q][:], gates[q][:], SILU)
+            hid_bfs.append(per_head.tile([P, TOKENS], BF16, name="hid_bf"))
+            nc.vector.tensor_tensor(hid_bfs[q][:], silus[q][:], ups[q][:], MULT)
+
+        hid_ts, owns = [], []
+        for q in range(HEADS):
+            hid_t_ps = psum_hid_t.tile([P, CHUNKS, P], BF16, name="hid_t_ps")
+            hid_by_chunk = hid_bfs[q][:].rearrange("c (p k) -> c k p", k=CHUNKS)
             for k in range(CHUNKS):
-                cols = slice(k * P, (k + 1) * P)
-                nc.tensor.transpose(hid_t_ps[:, cols], hid_bf[:, cols], identity[:])
-            hid_ts.append(per_head.tile([P, TOKENS], BF16, name="hid_t"))
+                nc.tensor.transpose(hid_t_ps[:, k, :], hid_by_chunk[:, k, :], identity_bf[:])
+            hid_ts.append(per_head.tile([P, CHUNKS, P], BF16, name="hid_t"))
             nc.scalar.copy(hid_ts[q][:], hid_t_ps[:])
+            owns.append(per_head.tile([P, TOKENS], F32, name="own"))
+            nc.vector.scalar_tensor_tensor(owns[q][:], silus[q][:], one_plus_eps[:, q : q + 1], ups[q][:], MULT, MULT)
 
         for q in range(HEADS):
             agg_ps = psum_agg.tile([P, TOKENS], F32, name="agg_ps")
             for k in range(CHUNKS):
-                nc.tensor.matmul(
-                    agg_ps[:], hid_ts[q][:, k * P : (k + 1) * P], adjs[q][:, k, :], start=(k == 0), stop=(k == CHUNKS - 1)
-                )
+                nc.tensor.matmul(agg_ps[:], hid_ts[q][:, k, :], adjs[q][:, k, :], start=(k == 0), stop=(k == CHUNKS - 1))
             mixed = per_head.tile([P, TOKENS], F32, name="mixed")
             nc.scalar.activation(mixed[:], agg_ps[:], COPY, scale=alpha_cols[:, q : q + 1])
             nc.vector.tensor_tensor(windows[q][:].indirect(offsets[:]), owns[q][:], mixed[:], ADD)

@@ -24,8 +24,9 @@ def tile_llamamlp_halfwaygin_kernel(tc, base, gate, up, adj_t, eps, alpha, offs,
         tc.psum_pool(name="psum_hid_t", bufs=2) as psum_hid_t,
         tc.psum_pool(name="psum_agg", bufs=HEADS) as psum_agg,
     ):
+        scale_rows = held.tile([SCALE_ROWS, P], F32, name="scale_rows")
+        nc.vector.memset(scale_rows[:], 0.0)
         offsets = held.tile([P, TOKENS // 16], U16, name="offsets")
-        nc.sync.dma_start(offsets[:], offs)
 
         head_rows = [slice(q * P, (q + 1) * P) for q in range(HEADS)]
         gates, ups, adjs, windows = [], [], [], []
@@ -34,16 +35,16 @@ def tile_llamamlp_halfwaygin_kernel(tc, base, gate, up, adj_t, eps, alpha, offs,
             ups.append(per_head.tile([P, TOKENS], F32, name="up_q"))
             nc.sync.dma_start(gates[q][:], gate[head_rows[q], :])
             nc.sync.dma_start(ups[q][:], up[head_rows[q], :])
+            if q == 0:
+                nc.sync.dma_start(scale_rows[0:HEADS, :], eps.rearrange("(q p) o -> q (p o)", p=P))
+                nc.sync.dma_start(scale_rows[HEADS : 2 * HEADS, :], alpha.rearrange("(q p) o -> q (p o)", p=P))
+        nc.sync.dma_start(offsets[:], offs)
         for q in range(HEADS):
             adjs.append(per_head.tile([P, CHUNKS, TOKENS], BF16, name="adj_q"))
             windows.append(per_head.tile([P, SLOTS], F32, name="window"))
             nc.sync.dma_start(adjs[q][:], adj_t[q].rearrange("(p k) j -> p k j", p=P))
             nc.sync.dma_start(windows[q][:], base[head_rows[q], :])
 
-        scale_rows = held.tile([SCALE_ROWS, P], F32, name="scale_rows")
-        nc.vector.memset(scale_rows[:], 0.0)
-        nc.scalar.dma_start(scale_rows[0:HEADS, :], eps.rearrange("(q p) o -> q (p o)", p=P))
-        nc.scalar.dma_start(scale_rows[HEADS : 2 * HEADS, :], alpha.rearrange("(q p) o -> q (p o)", p=P))
         identity_f32 = held.tile([SCALE_ROWS, SCALE_ROWS], F32, name="identity_f32")
         make_identity(nc, identity_f32[:])
         scale_cols_ps = psum_scales.tile([P, SCALE_ROWS], F32, name="scale_cols_ps")

@@ -10,6 +10,7 @@ HEADS = 4
 TOKENS = 512
 SLOTS = 2048
 CHUNKS = TOKENS // P
+HALF = TOKENS // 2
 SCALE_ROWS = 64
 
 FLOPS = 2 * HEADS * P * TOKENS * TOKENS
@@ -22,7 +23,7 @@ def tile_llamamlp_halfwaygin_kernel(tc, base, gate, up, adj_t, eps, alpha, offs,
         tc.tile_pool(name="per_head", bufs=HEADS) as per_head,
         tc.psum_pool(name="psum_scales", bufs=1) as psum_scales,
         tc.psum_pool(name="psum_hid_t", bufs=2) as psum_hid_t,
-        tc.psum_pool(name="psum_agg", bufs=HEADS) as psum_agg,
+        tc.psum_pool(name="psum_agg", bufs=4) as psum_agg,
     ):
         scale_rows = held.tile([SCALE_ROWS, P], F32, name="scale_rows")
         nc.vector.memset(scale_rows[:], 0.0)
@@ -76,10 +77,11 @@ def tile_llamamlp_halfwaygin_kernel(tc, base, gate, up, adj_t, eps, alpha, offs,
             nc.vector.scalar_tensor_tensor(owns[q][:], silus[q][:], one_plus_eps[:, q : q + 1], ups[q][:], MULT, MULT)
 
         for q in range(HEADS):
-            agg_ps = psum_agg.tile([P, TOKENS], F32, name="agg_ps")
-            for k in range(CHUNKS):
-                nc.tensor.matmul(agg_ps[:], hid_ts[q][:, k, :], adjs[q][:, k, :], start=(k == 0), stop=(k == CHUNKS - 1))
             mixed = per_head.tile([P, TOKENS], F32, name="mixed")
-            nc.scalar.activation(mixed[:], agg_ps[:], COPY, scale=alpha_cols[:, q : q + 1])
+            for half in (slice(0, HALF), slice(HALF, TOKENS)):
+                agg_ps = psum_agg.tile([P, HALF], F32, name="agg_ps")
+                for k in range(CHUNKS):
+                    nc.tensor.matmul(agg_ps[:], hid_ts[q][:, k, :], adjs[q][:, k, half], start=(k == 0), stop=(k == CHUNKS - 1))
+                nc.scalar.activation(mixed[:, half], agg_ps[:], COPY, scale=alpha_cols[:, q : q + 1])
             nc.vector.tensor_tensor(windows[q][:].indirect(offsets[:]), owns[q][:], mixed[:], ADD)
             nc.sync.dma_start(out[head_rows[q], :], windows[q][:])

@@ -7,6 +7,7 @@ SILU, COPY = mybir.ActivationFunctionType.Silu, mybir.ActivationFunctionType.Cop
 
 P = 128
 HEADS = 4
+LAST = HEADS - 1
 TOKENS = 512
 SLOTS = 2048
 CHUNKS = TOKENS // P
@@ -31,20 +32,35 @@ def tile_llamamlp_halfwaygin_kernel(tc, base, gate, up, adj_t, eps, alpha, offs,
 
         head_rows = [slice(q * P, (q + 1) * P) for q in range(HEADS)]
         gates, ups, adjs, windows = [], [], [], []
-        for q in range(HEADS):
+
+        def load_gate_up(q):
             gates.append(per_head.tile([P, TOKENS], F32, name="gate_q"))
             ups.append(per_head.tile([P, TOKENS], F32, name="up_q"))
             nc.sync.dma_start(gates[q][:], gate[head_rows[q], :])
             nc.sync.dma_start(ups[q][:], up[head_rows[q], :])
-            if q == 0:
-                nc.sync.dma_start(scale_rows[0:HEADS, :], eps.rearrange("(q p) o -> q (p o)", p=P))
-                nc.sync.dma_start(scale_rows[HEADS : 2 * HEADS, :], alpha.rearrange("(q p) o -> q (p o)", p=P))
-        nc.sync.dma_start(offsets[:], offs)
-        for q in range(HEADS):
+
+        def load_adj(q):
             adjs.append(per_head.tile([P, CHUNKS, TOKENS], BF16, name="adj_q"))
-            windows.append(per_head.tile([P, SLOTS], F32, name="window"))
             nc.sync.dma_start(adjs[q][:], adj_t[q].rearrange("(p k) j -> p k j", p=P))
+
+        def load_base(q):
+            windows.append(per_head.tile([P, SLOTS], F32, name="window"))
             nc.sync.dma_start(windows[q][:], base[head_rows[q], :])
+
+        load_gate_up(0)
+        nc.sync.dma_start(scale_rows[0:HEADS, :], eps.rearrange("(q p) o -> q (p o)", p=P))
+        nc.sync.dma_start(scale_rows[HEADS : 2 * HEADS, :], alpha.rearrange("(q p) o -> q (p o)", p=P))
+        for q in range(1, LAST):
+            load_gate_up(q)
+        nc.sync.dma_start(offsets[:], offs)
+        load_adj(0)
+        load_base(0)
+        load_adj(1)
+        load_gate_up(LAST)
+        load_base(1)
+        for q in range(2, HEADS):
+            load_adj(q)
+            load_base(q)
 
         identity_f32 = held.tile([SCALE_ROWS, SCALE_ROWS], F32, name="identity_f32")
         make_identity(nc, identity_f32[:])
@@ -58,25 +74,24 @@ def tile_llamamlp_halfwaygin_kernel(tc, base, gate, up, adj_t, eps, alpha, offs,
         identity_bf = held.tile([P, P], BF16, name="identity_bf")
         make_identity(nc, identity_bf[:])
 
-        silus, hid_bfs = [], []
-        for q in range(HEADS):
-            silus.append(per_head.tile([P, TOKENS], F32, name="silu_q"))
-            nc.scalar.activation(silus[q][:], gates[q][:], SILU)
-            hid_bfs.append(per_head.tile([P, TOKENS], BF16, name="hid_bf"))
-            nc.vector.tensor_tensor(hid_bfs[q][:], silus[q][:], ups[q][:], MULT)
+        def make_silu(q):
+            silu_q = per_head.tile([P, TOKENS], F32, name="silu_q")
+            nc.scalar.activation(silu_q[:], gates[q][:], SILU)
+            return silu_q
 
-        hid_ts, owns = [], []
-        for q in range(HEADS):
+        hid_ts = []
+
+        def flip(hid_bf):
             hid_t_ps = psum_hid_t.tile([P, CHUNKS, P], BF16, name="hid_t_ps")
-            hid_by_chunk = hid_bfs[q][:].rearrange("c (p k) -> c k p", k=CHUNKS)
+            hid_by_chunk = hid_bf[:].rearrange("c (p k) -> c k p", k=CHUNKS)
             for k in range(CHUNKS):
                 nc.tensor.transpose(hid_t_ps[:, k, :], hid_by_chunk[:, k, :], identity_bf[:])
             hid_ts.append(per_head.tile([P, CHUNKS, P], BF16, name="hid_t"))
-            nc.scalar.copy(hid_ts[q][:], hid_t_ps[:])
-            owns.append(per_head.tile([P, TOKENS], F32, name="own"))
-            nc.vector.scalar_tensor_tensor(owns[q][:], silus[q][:], one_plus_eps[:, q : q + 1], ups[q][:], MULT, MULT)
+            nc.scalar.copy(hid_ts[-1][:], hid_t_ps[:])
 
-        for q in range(HEADS):
+        owns = []
+
+        def mix_and_place(q):
             mixed = per_head.tile([P, TOKENS], F32, name="mixed")
             for half in (slice(0, HALF), slice(HALF, TOKENS)):
                 agg_ps = psum_agg.tile([P, HALF], F32, name="agg_ps")
@@ -85,3 +100,26 @@ def tile_llamamlp_halfwaygin_kernel(tc, base, gate, up, adj_t, eps, alpha, offs,
                 nc.scalar.activation(mixed[:, half], agg_ps[:], COPY, scale=alpha_cols[:, q : q + 1])
             nc.vector.tensor_tensor(windows[q][:].indirect(offsets[:]), owns[q][:], mixed[:], ADD)
             nc.sync.dma_start(out[head_rows[q], :], windows[q][:])
+
+        silus, hid_bfs = [], []
+        for q in range(LAST):
+            silus.append(make_silu(q))
+            hid_bfs.append(per_head.tile([P, TOKENS], BF16, name="hid_bf"))
+            nc.vector.tensor_tensor(hid_bfs[q][:], silus[q][:], ups[q][:], MULT)
+        for q in range(LAST):
+            flip(hid_bfs[q])
+            owns.append(per_head.tile([P, TOKENS], F32, name="own"))
+            nc.vector.scalar_tensor_tensor(owns[q][:], silus[q][:], one_plus_eps[:, q : q + 1], ups[q][:], MULT, MULT)
+        mix_and_place(0)
+
+        silu_last = make_silu(LAST)
+        hid_last = per_head.tile([P, TOKENS], F32, name="hid_last")
+        nc.vector.tensor_tensor(hid_last[:], silu_last[:], ups[LAST][:], MULT)
+        mix_and_place(1)
+        hid_bf_last = per_head.tile([P, TOKENS], BF16, name="hid_bf")
+        nc.scalar.copy(hid_bf_last[:], hid_last[:])
+        flip(hid_bf_last)
+        owns.append(per_head.tile([P, TOKENS], F32, name="own"))
+        nc.scalar.activation(owns[LAST][:], hid_last[:], COPY, scale=one_plus_eps[:, LAST : LAST + 1])
+        for q in range(2, HEADS):
+            mix_and_place(q)

import concourse.mybir as mybir
from concourse.masks import make_identity

F32, BF16, U16 = mybir.dt.float32, mybir.dt.bfloat16, mybir.dt.uint16
MULT, ADD = mybir.AluOpType.mult, mybir.AluOpType.add
SILU, COPY = mybir.ActivationFunctionType.Silu, mybir.ActivationFunctionType.Copy

P = 128
HEADS = 4
LAST = HEADS - 1
TOKENS = 512
SLOTS = 2048
CHUNKS = TOKENS // P
HALF = TOKENS // 2
SCALE_ROWS = 64

FLOPS = 2 * HEADS * P * TOKENS * TOKENS


def tile_llamamlp_halfwaygin_kernel(tc, base, gate, up, adj_t, eps, alpha, offs, out):
    nc = tc.nc
    with (
        tc.tile_pool(name="held", bufs=1) as held,
        tc.tile_pool(name="per_head", bufs=HEADS) as per_head,
        tc.psum_pool(name="psum_scales", bufs=1) as psum_scales,
        tc.psum_pool(name="psum_hid_t", bufs=2) as psum_hid_t,
        tc.psum_pool(name="psum_agg", bufs=4) as psum_agg,
    ):
        scale_rows = held.tile([SCALE_ROWS, P], F32, name="scale_rows")
        nc.vector.memset(scale_rows[:], 0.0)
        offsets = held.tile([P, TOKENS // 16], U16, name="offsets")

        head_rows = [slice(q * P, (q + 1) * P) for q in range(HEADS)]
        gates, ups, adjs, windows = [], [], [], []

        def load_gate_up(q):
            gates.append(per_head.tile([P, TOKENS], F32, name="gate_q"))
            ups.append(per_head.tile([P, TOKENS], F32, name="up_q"))
            nc.sync.dma_start(gates[q][:], gate[head_rows[q], :])
            nc.sync.dma_start(ups[q][:], up[head_rows[q], :])

        def load_adj(q):
            adjs.append(per_head.tile([P, CHUNKS, TOKENS], BF16, name="adj_q"))
            nc.sync.dma_start(adjs[q][:], adj_t[q].rearrange("(p k) j -> p k j", p=P))

        def load_base(q):
            windows.append(per_head.tile([P, SLOTS], F32, name="window"))
            nc.sync.dma_start(windows[q][:], base[head_rows[q], :])

        load_gate_up(0)
        nc.sync.dma_start(scale_rows[0:HEADS, :], eps.rearrange("(q p) o -> q (p o)", p=P))
        nc.sync.dma_start(scale_rows[HEADS : 2 * HEADS, :], alpha.rearrange("(q p) o -> q (p o)", p=P))
        for q in range(1, LAST):
            load_gate_up(q)
        nc.sync.dma_start(offsets[:], offs)
        load_adj(0)
        load_base(0)
        load_adj(1)
        load_gate_up(LAST)
        load_base(1)
        for q in range(2, HEADS):
            load_adj(q)
            load_base(q)

        identity_f32 = held.tile([SCALE_ROWS, SCALE_ROWS], F32, name="identity_f32")
        make_identity(nc, identity_f32[:])
        scale_cols_ps = psum_scales.tile([P, SCALE_ROWS], F32, name="scale_cols_ps")
        nc.tensor.transpose(scale_cols_ps[:], scale_rows[:], identity_f32[:])
        one_plus_eps = held.tile([P, HEADS], F32, name="one_plus_eps")
        nc.vector.tensor_scalar_add(one_plus_eps[:], scale_cols_ps[:, 0:HEADS], 1.0)
        alpha_cols = held.tile([P, HEADS], F32, name="alpha_cols")
        nc.vector.tensor_copy(alpha_cols[:], scale_cols_ps[:, HEADS : 2 * HEADS])

        identity_bf = held.tile([P, P], BF16, name="identity_bf")
        make_identity(nc, identity_bf[:])

        def make_silu(q):
            silu_q = per_head.tile([P, TOKENS], F32, name="silu_q")
            nc.scalar.activation(silu_q[:], gates[q][:], SILU)
            return silu_q

        hid_ts = []

        def flip(hid_bf):
            hid_t_ps = psum_hid_t.tile([P, CHUNKS, P], BF16, name="hid_t_ps")
            hid_by_chunk = hid_bf[:].rearrange("c (p k) -> c k p", k=CHUNKS)
            for k in range(CHUNKS):
                nc.tensor.transpose(hid_t_ps[:, k, :], hid_by_chunk[:, k, :], identity_bf[:])
            hid_ts.append(per_head.tile([P, CHUNKS, P], BF16, name="hid_t"))
            nc.scalar.copy(hid_ts[-1][:], hid_t_ps[:])

        owns = []

        def mix_and_place(q):
            mixed = per_head.tile([P, TOKENS], F32, name="mixed")
            for half in (slice(0, HALF), slice(HALF, TOKENS)):
                agg_ps = psum_agg.tile([P, HALF], F32, name="agg_ps")
                for k in range(CHUNKS):
                    nc.tensor.matmul(agg_ps[:], hid_ts[q][:, k, :], adjs[q][:, k, half], start=(k == 0), stop=(k == CHUNKS - 1))
                nc.scalar.activation(mixed[:, half], agg_ps[:], COPY, scale=alpha_cols[:, q : q + 1])
            nc.vector.tensor_tensor(windows[q][:].indirect(offsets[:]), owns[q][:], mixed[:], ADD)
            nc.sync.dma_start(out[head_rows[q], :], windows[q][:])

        silus, hid_bfs = [], []
        for q in range(LAST):
            silus.append(make_silu(q))
            hid_bfs.append(per_head.tile([P, TOKENS], BF16, name="hid_bf"))
            nc.vector.tensor_tensor(hid_bfs[q][:], silus[q][:], ups[q][:], MULT)
        for q in range(LAST):
            flip(hid_bfs[q])
            owns.append(per_head.tile([P, TOKENS], F32, name="own"))
            nc.vector.scalar_tensor_tensor(owns[q][:], silus[q][:], one_plus_eps[:, q : q + 1], ups[q][:], MULT, MULT)
        mix_and_place(0)

        silu_last = make_silu(LAST)
        hid_last = per_head.tile([P, TOKENS], F32, name="hid_last")
        nc.vector.tensor_tensor(hid_last[:], silu_last[:], ups[LAST][:], MULT)
        mix_and_place(1)
        hid_bf_last = per_head.tile([P, TOKENS], BF16, name="hid_bf")
        nc.scalar.copy(hid_bf_last[:], hid_last[:])
        flip(hid_bf_last)
        owns.append(per_head.tile([P, TOKENS], F32, name="own"))
        nc.scalar.activation(owns[LAST][:], hid_last[:], COPY, scale=one_plus_eps[:, LAST : LAST + 1])
        for q in range(2, HEADS):
            mix_and_place(q)
